import numpy as np
import ml_dtypes


def mxq(x, axis, fmt="e4m3"):
    dtype, down = {"e4m3": (ml_dtypes.float8_e4m3fn, 7), "e5m2": (ml_dtypes.float8_e5m2, 14)}[fmt]
    v = np.moveaxis(np.asarray(x, np.float32).astype(ml_dtypes.bfloat16).astype(np.float64), axis, -1)
    blocks = v.reshape(v.shape[:-1] + (-1, 32))
    amax = np.abs(blocks).max(-1, keepdims=True)
    byte = np.maximum(np.where(amax > 0, np.frexp(amax)[1] - 1 + 127, 0) - down, 1)
    scale = np.exp2(byte - 127.0)
    codes = (blocks / scale).astype(np.float32).astype(dtype).astype(np.float64)
    return np.moveaxis((codes * scale).reshape(v.shape), -1, axis)


WIDE = False


def mx_kscale(k):
    if not WIDE:
        return np.ones(k)
    levels = np.array([10, -10, 5, -5, 0])
    a = np.random.permutation(np.resize(levels, k // 512 * 4)).reshape(k // 512, 4)
    idx = np.arange(k)
    return np.exp2(a[idx // 512, idx % 128 // 32])


BF16 = ml_dtypes.bfloat16


def bf(x):
    return np.asarray(x, np.float32).astype(BF16)


def f64(x):
    return np.asarray(x).astype(np.float64)


E2M1 = np.array([0.0, 0.5, 1.0, 1.5, 2.0, 3.0, 4.0, 6.0, -0.0, -0.5, -1.0, -1.5, -2.0, -3.0, -4.0, -6.0])


def pack_weight(w, fmt):
    k, n = w.shape
    w = f64(bf(w)).reshape(k // 32, 32, n)
    amax = np.abs(w).max(1)
    if fmt == "e4m3":
        byte = np.frexp(amax)[1] - 1 + 127 - 7
    else:
        mant, ex = np.frexp(amax / 6.0)
        byte = np.where(mant > 0.5, ex, ex - 1) + 127
    byte = np.clip(np.where(amax > 0, byte, 1), 1, 254)
    scaled = (w * np.exp2(127.0 - byte)[:, None, :]).reshape(k, n).astype(np.float32)
    by_word = np.ascontiguousarray(scaled.reshape(k // 512, 128, 4, n).transpose(0, 1, 3, 2))
    if fmt == "e4m3":
        words = by_word.astype(ml_dtypes.float8_e4m3fn).view(np.uint8)
    else:
        c = by_word.astype(ml_dtypes.float4_e2m1fn).view(np.uint8) & 0xF
        words = c[..., 0::2] | (c[..., 1::2] << 4)
    return np.ascontiguousarray(words), np.ascontiguousarray(byte.astype(np.uint8).reshape(k // 512, 16, n))


def unpack_weight(words, scales, fmt):
    g, p, n, _ = words.shape
    if fmt == "e4m3":
        vals = np.ascontiguousarray(words).view(ml_dtypes.float8_e4m3fn).astype(np.float64)
    else:
        nib = np.empty((g, p, n, 4), np.uint8)
        nib[..., 0::2] = words & 0xF
        nib[..., 1::2] = words >> 4
        vals = E2M1[nib]
    vals = vals * np.repeat(np.exp2(scales.astype(np.float64) - 127.0), 8, axis=1)[..., None]
    return vals.transpose(0, 1, 3, 2).reshape(g * 512, n)


N, P, D, E, F = 256, 3, 512, 16384, 256
BN_EPS = 1e-5


def setup_inputs():
    t = mx_kscale(E)
    h = 1.2 * np.random.standard_normal((N, P, E)) + 0.6 * np.random.standard_normal((1, P, E))
    w1b_words, w1b_scales = pack_weight(np.random.standard_normal((E, F)) / np.sqrt(E) / t[:, None], "e4m3")
    w2b_words, w2b_scales = pack_weight(np.random.standard_normal((E, F)) / np.sqrt(E) / t[:, None], "e4m3")
    return {"h_sage": bf(h * t),
            "w1b_words": w1b_words,
            "w1b_scales": w1b_scales,
            "w2b_words": w2b_words,
            "w2b_scales": w2b_scales,
            "gamma": bf(1.0 + 0.2 * np.random.standard_normal(F)),
            "beta": bf(0.3 * np.random.standard_normal(F))}


def reference(h_sage, w1b_words, w1b_scales, w2b_words, w2b_scales, gamma, beta):
    h = f64(h_sage)
    neigh = (h.sum(axis=1, keepdims=True) - h) * 0.5
    out = (mxq(h[:, 0, :], 1, "e4m3") @ unpack_weight(w2b_words, w2b_scales, "e4m3")) + (mxq(neigh[:, 0, :], 1, "e4m3") @ unpack_weight(w1b_words, w1b_scales, "e4m3"))
    mean = out.mean(axis=0)
    var = out.var(axis=0)
    out = (out - mean) / np.sqrt(var + BN_EPS) * f64(gamma) + f64(beta)
    return 1.0 / (1.0 + np.exp(-out))

@@ -1,0 +1,197 @@
+import concourse.mybir as mybir
+from concourse.masks import make_identity
+
+FLOPS = 2 * 2 * 256 * 16384 * 256
+
+F32 = mybir.dt.float32
+BF16 = mybir.dt.bfloat16
+I32 = mybir.dt.int32
+U32 = mybir.dt.uint32
+U8 = mybir.dt.uint8
+FP8X4 = mybir.dt.float8_e4m3fn_x4
+ALU = mybir.AluOpType
+ACT = mybir.ActivationFunctionType
+
+P = 128
+ITEMS = 256
+ITEM_TILES = ITEMS // P
+FEATURES = 16384
+COLS = 256
+COL_HALVES = COLS // P
+GROUP = 4 * P
+GROUPS = FEATURES // GROUP
+GROUP_WORDS = GROUP // 2
+CHUNK = 4096
+CHUNKS = FEATURES // CHUNK
+CHUNK_GROUPS = CHUNK // GROUP
+BANK_GROUPS = 2
+PIECE_GROUPS = 4
+SCALE_ROWS = 4
+BN_EPS = 1e-5
+
+SELF = 0
+NEIGH = 1
+
+
+def tile_dogtaitujuanji_pb_k_kernel(
+    tc, h_sage, w1b_words, w1b_scales, w2b_words, w2b_scales, gamma, beta, out
+):
+    nc = tc.nc
+    weight_words = {SELF: w2b_words, NEIGH: w1b_words}
+    weight_scales = {SELF: w2b_scales, NEIGH: w1b_scales}
+
+    with tc.tile_pool(name="keep", bufs=1) as keep, tc.tile_pool(name="hops", bufs=4) as hops, tc.tile_pool(
+        name="stage", bufs=4
+    ) as stage, tc.tile_pool(name="weights", bufs=6) as weights, tc.psum_pool(
+        name="sums", bufs=1
+    ) as sums, tc.psum_pool(name="turn", bufs=4) as turn:
+        ident = keep.tile([P, P], F32)
+        make_identity(nc, ident[:])
+
+        zero_col = keep.tile([P, 1], F32)
+        nc.vector.memset(zero_col[:], 0.0)
+        table_warm = keep.tile([P, 1], F32)
+        nc.scalar.activation(out=table_warm[:], in_=zero_col[:], func=ACT.Sigmoid)
+
+        neg_half = keep.tile([P, COL_HALVES], F32)
+        nc.vector.memset(neg_half[:], -0.5)
+
+        rows_bf = keep.tile([P, P], BF16)
+        nc.vector.memset(rows_bf[:], 0.0)
+        nc.gpsimd.dma_start(out=rows_bf[0:COL_HALVES, :], in_=gamma.rearrange("(h c) -> h c", h=COL_HALVES))
+        nc.gpsimd.dma_start(
+            out=rows_bf[COL_HALVES : 2 * COL_HALVES, :], in_=beta.rearrange("(h c) -> h c", h=COL_HALVES)
+        )
+
+        w_planes = keep.tile([P, 2, GROUPS, COLS], U8, align_bytes=64)
+        nc.vector.memset(w_planes[:].bitcast(I32), 0)
+        for operand in (SELF, NEIGH):
+            by_row = weight_scales[operand].bitcast(F32).rearrange("g (q r) c -> r q g c", r=SCALE_ROWS)
+            for r in range(SCALE_ROWS):
+                nc.gpsimd.dma_start(out=w_planes[:].bitcast(F32)[r:P:32, operand, :, :], in_=by_row[r])
+
+        x_codes = {}
+        x_planes = {}
+        for operand in (SELF, NEIGH):
+            for c in range(CHUNKS):
+                x_codes[operand, c] = keep.tile(
+                    [P, CHUNK_GROUPS, ITEMS], U32, name="x_codes_%d_%d" % (operand, c), align_bytes=64
+                )
+                x_planes[operand, c] = keep.tile(
+                    [P, CHUNK_GROUPS, ITEMS], U8, name="x_planes_%d_%d" % (operand, c), align_bytes=64
+                )
+
+        for c in range(CHUNKS):
+            features = slice(c * CHUNK, (c + 1) * CHUNK)
+            for it in range(ITEM_TILES):
+                items = slice(it * P, (it + 1) * P)
+                neighbours = hops.tile([P, 2, CHUNK], BF16)
+                nc.sync.dma_start(out=neighbours[:], in_=h_sage[items, 1:3, features])
+                own = hops.tile([P, CHUNK], BF16)
+                nc.sync.dma_start(out=own[:], in_=h_sage[items, 0, features])
+
+                nc.vector.tensor_tensor(
+                    out=neighbours[:, 0, :], in0=neighbours[:, 0, :], in1=neighbours[:, 1, :], op=ALU.add
+                )
+
+                for operand, values in ((SELF, own[:]), (NEIGH, neighbours[:, 0, :])):
+                    words = values.bitcast(F32)
+                    for first in range(0, CHUNK_GROUPS, BANK_GROUPS):
+                        turned = turn.tile([P, BANK_GROUPS, 2, P], F32)
+                        for j in range(BANK_GROUPS):
+                            start_word = (first + j) * GROUP_WORDS
+                            for u in range(2):
+                                nc.tensor.transpose(
+                                    turned[:, j, u, :],
+                                    words[:, start_word + u : start_word + GROUP_WORDS : 2],
+                                    ident[:],
+                                )
+                        grouped = stage.tile([P, BANK_GROUPS, 4 * P], BF16, align_bytes=64)
+                        nc.scalar.copy(
+                            out=grouped[:].bitcast(F32).rearrange("p j (i u) -> p j i u", u=2),
+                            in_=turned[:].rearrange("p j u i -> p j i u"),
+                        )
+                        for j in range(BANK_GROUPS):
+                            nc.vector.quantize_mx(
+                                out=x_codes[operand, c][:, first + j, items].bitcast(FP8X4),
+                                scales=x_planes[operand, c][:, first + j, items],
+                                in_=grouped[:, j, :],
+                            )
+
+        rows_f32 = keep.tile([P, P], F32)
+        nc.vector.tensor_copy(out=rows_f32[:], in_=rows_bf[:])
+        cols_ps = turn.tile([P, P], F32, tag="turned")
+        nc.tensor.transpose(cols_ps[:], rows_f32[:], ident[:])
+        gamma_beta = keep.tile([P, 2 * COL_HALVES], F32)
+        nc.vector.tensor_copy(out=gamma_beta[:], in_=cols_ps[:, 0 : 2 * COL_HALVES])
+
+        product = {}
+        for operand in (SELF, NEIGH):
+            for h in range(COL_HALVES):
+                product[operand, h] = sums.tile([P, ITEMS], F32, name="product_%d_%d" % (operand, h))
+
+        self_sb = keep.tile([P, COL_HALVES, ITEMS], F32)
+        for operand in (SELF, NEIGH):
+            for first in range(0, GROUPS, PIECE_GROUPS):
+                piece = weights.tile([P, PIECE_GROUPS, COLS], U32, align_bytes=64)
+                nc.sync.dma_start(
+                    out=piece[:].bitcast(I32),
+                    in_=weight_words[operand][first : first + PIECE_GROUPS]
+                    .rearrange("g p c t -> p g (c t)")
+                    .bitcast(I32),
+                )
+                for h in range(COL_HALVES):
+                    cols = slice(h * P, (h + 1) * P)
+                    for j in range(PIECE_GROUPS):
+                        g = first + j
+                        nc.tensor.matmul_mx(
+                            out=product[operand, h][:],
+                            lhsT=piece[:, j, cols].bitcast(FP8X4),
+                            lhsT_scale=w_planes[:, operand, g, cols],
+                            rhs=x_codes[operand, g // CHUNK_GROUPS][:, g % CHUNK_GROUPS, :].bitcast(FP8X4),
+                            rhs_scale=x_planes[operand, g // CHUNK_GROUPS][:, g % CHUNK_GROUPS, :],
+                            start=(g == 0),
+                            stop=(g == GROUPS - 1),
+                        )
+            if operand == SELF:
+                for h in range(COL_HALVES):
+                    nc.scalar.copy(out=self_sb[:, h, :], in_=product[SELF, h][:])
+
+        y = keep.tile([P, COL_HALVES, ITEMS], F32)
+        stats = keep.tile([P, COL_HALVES, 6], F32)
+        mean_var = keep.tile([P, COL_HALVES, 2], F32)
+        for h in range(COL_HALVES):
+            nc.vector.scalar_tensor_tensor(
+                out=y[:, h, :], in0=product[NEIGH, h][:], scalar=0.5, in1=self_sb[:, h, :], op0=ALU.mult, op1=ALU.add
+            )
+            nc.vector.bn_stats(out=stats[:, h, :], in_=y[:, h, :])
+            nc.vector.bn_aggr(out=mean_var[:, h, :], in_=stats[:, h, :])
+
+        var_eps = keep.tile([P, COL_HALVES], F32)
+        nc.vector.tensor_scalar(out=var_eps[:], in0=mean_var[:, :, 1], scalar1=BN_EPS, scalar2=None, op0=ALU.add)
+        rstd = keep.tile([P, COL_HALVES], F32)
+        nc.gpsimd.tensor_tensor(out=rstd[:], in0=var_eps[:], in1=neg_half[:], op=ALU.pow)
+        gain = keep.tile([P, COL_HALVES], F32)
+        nc.vector.tensor_tensor(out=gain[:], in0=rstd[:], in1=gamma_beta[:, 0:COL_HALVES], op=ALU.mult)
+        mean_gain = keep.tile([P, COL_HALVES], F32)
+        nc.vector.tensor_tensor(out=mean_gain[:], in0=mean_var[:, :, 0], in1=gain[:], op=ALU.mult)
+        shift = keep.tile([P, COL_HALVES], F32)
+        nc.vector.tensor_tensor(
+            out=shift[:], in0=gamma_beta[:, COL_HALVES : 2 * COL_HALVES], in1=mean_gain[:], op=ALU.subtract
+        )
+        for h in range(COL_HALVES):
+            nc.scalar.activation(
+                out=y[:, h, :], in_=y[:, h, :], func=ACT.Sigmoid, bias=shift[:, h : h + 1], scale=gain[:, h : h + 1]
+            )
+
+        result = keep.tile([P, ITEM_TILES, COLS], F32)
+        for it in range(ITEM_TILES):
+            items = slice(it * P, (it + 1) * P)
+            back = turn.tile([P, COLS], F32, tag="turned")
+            for h in range(COL_HALVES):
+                nc.tensor.transpose(back[:, h * P : (h + 1) * P], y[:, h, items], ident[:])
+            if it == 0:
+                nc.vector.tensor_copy(out=result[:, it, :], in_=back[:])
+            else:
+                nc.scalar.copy(out=result[:, it, :], in_=back[:])
+            nc.sync.dma_start(out=out[items, :], in_=result[:, it, :])

@@ -42,7 +42,7 @@ def tile_dogtaitujuanji_pb_k_kernel(
 
     with tc.tile_pool(name="keep", bufs=1) as keep, tc.tile_pool(name="hops", bufs=4) as hops, tc.tile_pool(
         name="stage", bufs=4
-    ) as stage, tc.tile_pool(name="weights", bufs=6) as weights, tc.psum_pool(
+    ) as stage, tc.tile_pool(name="weights", bufs=8) as weights, tc.psum_pool(
         name="sums", bufs=1
     ) as sums, tc.psum_pool(name="turn", bufs=4) as turn:
         ident = keep.tile([P, P], F32)
@@ -53,22 +53,18 @@ def tile_dogtaitujuanji_pb_k_kernel(
         table_warm = keep.tile([P, 1], F32)
         nc.scalar.activation(out=table_warm[:], in_=zero_col[:], func=ACT.Sigmoid)
 
-        neg_half = keep.tile([P, COL_HALVES], F32)
+        neg_half = keep.tile([P, 1], F32)
         nc.vector.memset(neg_half[:], -0.5)
 
         rows_bf = keep.tile([P, P], BF16)
         nc.vector.memset(rows_bf[:], 0.0)
-        nc.gpsimd.dma_start(out=rows_bf[0:COL_HALVES, :], in_=gamma.rearrange("(h c) -> h c", h=COL_HALVES))
-        nc.gpsimd.dma_start(
-            out=rows_bf[COL_HALVES : 2 * COL_HALVES, :], in_=beta.rearrange("(h c) -> h c", h=COL_HALVES)
-        )
 
-        w_planes = keep.tile([P, 2, GROUPS, COLS], U8, align_bytes=64)
+        w_planes = keep.tile([P, GROUPS, COLS], U8, align_bytes=256)
         nc.vector.memset(w_planes[:].bitcast(I32), 0)
         for operand in (SELF, NEIGH):
             by_row = weight_scales[operand].bitcast(F32).rearrange("g (q r) c -> r q g c", r=SCALE_ROWS)
             for r in range(SCALE_ROWS):
-                nc.gpsimd.dma_start(out=w_planes[:].bitcast(F32)[r:P:32, operand, :, :], in_=by_row[r])
+                nc.gpsimd.dma_start(out=w_planes[:].bitcast(F32)[SCALE_ROWS * operand + r : P : 32, :, :], in_=by_row[r])
 
         x_codes = {}
         x_planes = {}
@@ -85,9 +81,9 @@ def tile_dogtaitujuanji_pb_k_kernel(
             features = slice(c * CHUNK, (c + 1) * CHUNK)
             for it in range(ITEM_TILES):
                 items = slice(it * P, (it + 1) * P)
-                neighbours = hops.tile([P, 2, CHUNK], BF16)
+                neighbours = hops.tile([P, 2, CHUNK], BF16, align_bytes=256)
                 nc.sync.dma_start(out=neighbours[:], in_=h_sage[items, 1:3, features])
-                own = hops.tile([P, CHUNK], BF16)
+                own = hops.tile([P, CHUNK], BF16, align_bytes=256)
                 nc.sync.dma_start(out=own[:], in_=h_sage[items, 0, features])
 
                 nc.vector.tensor_tensor(
@@ -118,6 +114,10 @@ def tile_dogtaitujuanji_pb_k_kernel(
                                 in_=grouped[:, j, :],
                             )
 
+        nc.sync.dma_start(out=rows_bf[0:COL_HALVES, :], in_=gamma.rearrange("(h c) -> h c", h=COL_HALVES))
+        nc.sync.dma_start(
+            out=rows_bf[COL_HALVES : 2 * COL_HALVES, :], in_=beta.rearrange("(h c) -> h c", h=COL_HALVES)
+        )
         rows_f32 = keep.tile([P, P], F32)
         nc.vector.tensor_copy(out=rows_f32[:], in_=rows_bf[:])
         cols_ps = turn.tile([P, P], F32, tag="turned")
@@ -131,67 +131,83 @@ def tile_dogtaitujuanji_pb_k_kernel(
                 product[operand, h] = sums.tile([P, ITEMS], F32, name="product_%d_%d" % (operand, h))
 
         self_sb = keep.tile([P, COL_HALVES, ITEMS], F32)
-        for operand in (SELF, NEIGH):
-            for first in range(0, GROUPS, PIECE_GROUPS):
-                piece = weights.tile([P, PIECE_GROUPS, COLS], U32, align_bytes=64)
-                nc.sync.dma_start(
-                    out=piece[:].bitcast(I32),
-                    in_=weight_words[operand][first : first + PIECE_GROUPS]
-                    .rearrange("g p c t -> p g (c t)")
-                    .bitcast(I32),
-                )
-                for h in range(COL_HALVES):
-                    cols = slice(h * P, (h + 1) * P)
-                    for j in range(PIECE_GROUPS):
-                        g = first + j
-                        nc.tensor.matmul_mx(
-                            out=product[operand, h][:],
-                            lhsT=piece[:, j, cols].bitcast(FP8X4),
-                            lhsT_scale=w_planes[:, operand, g, cols],
-                            rhs=x_codes[operand, g // CHUNK_GROUPS][:, g % CHUNK_GROUPS, :].bitcast(FP8X4),
-                            rhs_scale=x_planes[operand, g // CHUNK_GROUPS][:, g % CHUNK_GROUPS, :],
-                            start=(g == 0),
-                            stop=(g == GROUPS - 1),
-                        )
-            if operand == SELF:
+        pieces = [(operand, first, PIECE_GROUPS) for operand in (SELF, NEIGH) for first in range(0, GROUPS, PIECE_GROUPS)]
+        operand, first, count = pieces[-1]
+        pieces[-1:] = [(operand, first, count // 2), (operand, first + count // 2, count // 2)]
+        for operand, first, count in pieces:
+            piece = weights.tile([P, PIECE_GROUPS, COLS], U32, align_bytes=256)
+            nc.sync.dma_start(
+                out=piece[:, 0:count, :].bitcast(I32),
+                in_=weight_words[operand][first : first + count]
+                .rearrange("g p c t -> p g (c t)")
+                .bitcast(I32),
+            )
+            for h in range(COL_HALVES):
+                cols = slice(h * P, (h + 1) * P)
+                for j in range(count):
+                    g = first + j
+                    nc.tensor.matmul_mx(
+                        out=product[operand, h][:],
+                        lhsT=piece[:, j, cols].bitcast(FP8X4),
+                        lhsT_scale=w_planes[SCALE_ROWS * operand : P, g, cols],
+                        rhs=x_codes[operand, g // CHUNK_GROUPS][:, g % CHUNK_GROUPS, :].bitcast(FP8X4),
+                        rhs_scale=x_planes[operand, g // CHUNK_GROUPS][:, g % CHUNK_GROUPS, :],
+                        start=(g == 0),
+                        stop=(g == GROUPS - 1),
+                    )
+            if operand == SELF and first + count == GROUPS:
                 for h in range(COL_HALVES):
                     nc.scalar.copy(out=self_sb[:, h, :], in_=product[SELF, h][:])
 
-        y = keep.tile([P, COL_HALVES, ITEMS], F32)
-        stats = keep.tile([P, COL_HALVES, 6], F32)
-        mean_var = keep.tile([P, COL_HALVES, 2], F32)
+        y = {}
+        mean_var = {}
+        rstd = {}
+        minus_mean_gamma = {}
         for h in range(COL_HALVES):
+            y[h] = keep.tile([P, ITEMS], F32, name="y_%d" % h)
             nc.vector.scalar_tensor_tensor(
-                out=y[:, h, :], in0=product[NEIGH, h][:], scalar=0.5, in1=self_sb[:, h, :], op0=ALU.mult, op1=ALU.add
+                out=y[h][:], in0=product[NEIGH, h][:], scalar=0.5, in1=self_sb[:, h, :], op0=ALU.mult, op1=ALU.add
             )
-            nc.vector.bn_stats(out=stats[:, h, :], in_=y[:, h, :])
-            nc.vector.bn_aggr(out=mean_var[:, h, :], in_=stats[:, h, :])
-
-        var_eps = keep.tile([P, COL_HALVES], F32)
-        nc.vector.tensor_scalar(out=var_eps[:], in0=mean_var[:, :, 1], scalar1=BN_EPS, scalar2=None, op0=ALU.add)
-        rstd = keep.tile([P, COL_HALVES], F32)
-        nc.gpsimd.tensor_tensor(out=rstd[:], in0=var_eps[:], in1=neg_half[:], op=ALU.pow)
-        gain = keep.tile([P, COL_HALVES], F32)
-        nc.vector.tensor_tensor(out=gain[:], in0=rstd[:], in1=gamma_beta[:, 0:COL_HALVES], op=ALU.mult)
-        mean_gain = keep.tile([P, COL_HALVES], F32)
-        nc.vector.tensor_tensor(out=mean_gain[:], in0=mean_var[:, :, 0], in1=gain[:], op=ALU.mult)
-        shift = keep.tile([P, COL_HALVES], F32)
-        nc.vector.tensor_tensor(
-            out=shift[:], in0=gamma_beta[:, COL_HALVES : 2 * COL_HALVES], in1=mean_gain[:], op=ALU.subtract
-        )
+            stats = keep.tile([P, 6], F32, name="stats_%d" % h)
+            nc.vector.bn_stats(out=stats[:], in_=y[h][:])
+            mean_var[h] = keep.tile([P, 2], F32, name="mean_var_%d" % h)
+            nc.vector.bn_aggr(out=mean_var[h][:], in_=stats[:])
+            var_eps = keep.tile([P, 1], F32, name="var_eps_%d" % h)
+            nc.vector.tensor_scalar(
+                out=var_eps[:], in0=mean_var[h][:, 1:2], scalar1=BN_EPS, scalar2=None, op0=ALU.add
+            )
+            rstd[h] = keep.tile([P, 1], F32, name="rstd_%d" % h)
+            nc.gpsimd.tensor_tensor(out=rstd[h][:], in0=var_eps[:], in1=neg_half[:], op=ALU.pow)
+            minus_mean_gamma[h] = keep.tile([P, 1], F32, name="minus_mean_gamma_%d" % h)
+            nc.vector.scalar_tensor_tensor(
+                out=minus_mean_gamma[h][:],
+                in0=mean_var[h][:, 0:1],
+                scalar=-1.0,
+                in1=gamma_beta[:, h : h + 1],
+                op0=ALU.mult,
+                op1=ALU.mult,
+            )
+        by_half = out.rearrange("(it p) (h c) -> h p it c", p=P, c=P)
         for h in range(COL_HALVES):
-            nc.scalar.activation(
-                out=y[:, h, :], in_=y[:, h, :], func=ACT.Sigmoid, bias=shift[:, h : h + 1], scale=gain[:, h : h + 1]
+            gain = keep.tile([P, 1], F32, name="gain_%d" % h)
+            nc.vector.tensor_tensor(out=gain[:], in0=rstd[h][:], in1=gamma_beta[:, h : h + 1], op=ALU.mult)
+            shift = keep.tile([P, 1], F32, name="shift_%d" % h)
+            nc.vector.scalar_tensor_tensor(
+                out=shift[:],
+                in0=minus_mean_gamma[h][:],
+                scalar=rstd[h][:],
+                in1=gamma_beta[:, COL_HALVES + h : COL_HALVES + h + 1],
+                op0=ALU.mult,
+                op1=ALU.add,
             )
+            nc.scalar.activation(out=y[h][:], in_=y[h][:], func=ACT.Sigmoid, bias=shift[:], scale=gain[:])
 
-        result = keep.tile([P, ITEM_TILES, COLS], F32)
-        for it in range(ITEM_TILES):
-            items = slice(it * P, (it + 1) * P)
-            back = turn.tile([P, COLS], F32, tag="turned")
-            for h in range(COL_HALVES):
-                nc.tensor.transpose(back[:, h * P : (h + 1) * P], y[:, h, items], ident[:])
-            if it == 0:
-                nc.vector.tensor_copy(out=result[:, it, :], in_=back[:])
-            else:
-                nc.scalar.copy(out=result[:, it, :], in_=back[:])
-            nc.sync.dma_start(out=out[items, :], in_=result[:, it, :])
+            result = keep.tile([P, ITEM_TILES, P], F32, name="result_%d" % h)
+            for it in range(ITEM_TILES):
+                back = turn.tile([P, P], F32, tag="turned")
+                nc.tensor.transpose(back[:], y[h][:, it * P : (it + 1) * P], ident[:])
+                if it == 0:
+                    nc.vector.tensor_copy(out=result[:, it, :], in_=back[:])
+                else:
+                    nc.scalar.copy(out=result[:, it, :], in_=back[:])
+            nc.sync.dma_start(out=by_half[h], in_=result[:])

@@ -53,7 +53,7 @@ def tile_dogtaitujuanji_pb_k_kernel(
         table_warm = keep.tile([P, 1], F32)
         nc.scalar.activation(out=table_warm[:], in_=zero_col[:], func=ACT.Sigmoid)
 
-        neg_half = keep.tile([P, 1], F32)
+        neg_half = keep.tile([P, COL_HALVES], F32)
         nc.vector.memset(neg_half[:], -0.5)
 
         rows_bf = keep.tile([P, P], BF16)
@@ -61,20 +61,25 @@ def tile_dogtaitujuanji_pb_k_kernel(
 
         w_planes = keep.tile([P, GROUPS, COLS], U8, align_bytes=256)
         nc.vector.memset(w_planes[:].bitcast(I32), 0)
-        for operand in (SELF, NEIGH):
-            by_row = weight_scales[operand].bitcast(F32).rearrange("g (q r) c -> r q g c", r=SCALE_ROWS)
-            for r in range(SCALE_ROWS):
-                nc.gpsimd.dma_start(out=w_planes[:].bitcast(F32)[SCALE_ROWS * operand + r : P : 32, :, :], in_=by_row[r])
+        scale_rows = [(operand, q) for operand in (SELF, NEIGH) for q in range(4 * SCALE_ROWS)]
+
+        def load_scale_rows(rows):
+            for operand, q in rows:
+                p = 32 * (q // SCALE_ROWS) + q % SCALE_ROWS + SCALE_ROWS * operand
+                nc.sync.dma_start(
+                    out=w_planes[p : p + 1, :, :].bitcast(I32),
+                    in_=weight_scales[operand][:, q : q + 1, :].rearrange("g q c -> q g c").bitcast(I32),
+                )
 
         x_codes = {}
         x_planes = {}
         for operand in (SELF, NEIGH):
             for c in range(CHUNKS):
                 x_codes[operand, c] = keep.tile(
-                    [P, CHUNK_GROUPS, ITEMS], U32, name="x_codes_%d_%d" % (operand, c), align_bytes=64
+                    [P, CHUNK_GROUPS, ITEMS], U32, name="x_codes_%d_%d" % (operand, c), align_bytes=256
                 )
                 x_planes[operand, c] = keep.tile(
-                    [P, CHUNK_GROUPS, ITEMS], U8, name="x_planes_%d_%d" % (operand, c), align_bytes=64
+                    [P, CHUNK_GROUPS, ITEMS], U8, name="x_planes_%d_%d" % (operand, c), align_bytes=256
                 )
 
         for c in range(CHUNKS):
@@ -83,6 +88,8 @@ def tile_dogtaitujuanji_pb_k_kernel(
                 items = slice(it * P, (it + 1) * P)
                 neighbours = hops.tile([P, 2, CHUNK], BF16, align_bytes=256)
                 nc.sync.dma_start(out=neighbours[:], in_=h_sage[items, 1:3, features])
+                load_scale_rows(scale_rows[:4])
+                scale_rows = scale_rows[4:]
                 own = hops.tile([P, CHUNK], BF16, align_bytes=256)
                 nc.sync.dma_start(out=own[:], in_=h_sage[items, 0, features])
 
@@ -102,7 +109,7 @@ def tile_dogtaitujuanji_pb_k_kernel(
                                     words[:, start_word + u : start_word + GROUP_WORDS : 2],
                                     ident[:],
                                 )
-                        grouped = stage.tile([P, BANK_GROUPS, 4 * P], BF16, align_bytes=64)
+                        grouped = stage.tile([P, BANK_GROUPS, 4 * P], BF16, align_bytes=256)
                         nc.scalar.copy(
                             out=grouped[:].bitcast(F32).rearrange("p j (i u) -> p j i u", u=2),
                             in_=turned[:].rearrange("p j u i -> p j i u"),
@@ -160,49 +167,44 @@ def tile_dogtaitujuanji_pb_k_kernel(
                     nc.scalar.copy(out=self_sb[:, h, :], in_=product[SELF, h][:])
 
         y = {}
-        mean_var = {}
-        rstd = {}
-        minus_mean_gamma = {}
-        for h in range(COL_HALVES):
+        stats = {}
+        mean_var = keep.tile([P, COL_HALVES, 2], F32)
+        var_eps = keep.tile([P, COL_HALVES], F32)
+        rstd = keep.tile([P, COL_HALVES], F32)
+        halves = range(COL_HALVES)
+        for h in halves:
             y[h] = keep.tile([P, ITEMS], F32, name="y_%d" % h)
             nc.vector.scalar_tensor_tensor(
                 out=y[h][:], in0=product[NEIGH, h][:], scalar=0.5, in1=self_sb[:, h, :], op0=ALU.mult, op1=ALU.add
             )
-            stats = keep.tile([P, 6], F32, name="stats_%d" % h)
-            nc.vector.bn_stats(out=stats[:], in_=y[h][:])
-            mean_var[h] = keep.tile([P, 2], F32, name="mean_var_%d" % h)
-            nc.vector.bn_aggr(out=mean_var[h][:], in_=stats[:])
-            var_eps = keep.tile([P, 1], F32, name="var_eps_%d" % h)
+        for h in halves:
+            stats[h] = keep.tile([P, 6], F32, name="stats_%d" % h)
+            nc.vector.bn_stats(out=stats[h][:], in_=y[h][:])
+        for h in halves:
+            nc.vector.bn_aggr(out=mean_var[:, h, :], in_=stats[h][:])
+        nc.vector.tensor_scalar(out=var_eps[:], in0=mean_var[:, :, 1], scalar1=BN_EPS, scalar2=None, op0=ALU.add)
+        nc.gpsimd.tensor_tensor(out=rstd[:], in0=var_eps[:], in1=neg_half[:], op=ALU.pow)
+        for h in halves:
             nc.vector.tensor_scalar(
-                out=var_eps[:], in0=mean_var[h][:, 1:2], scalar1=BN_EPS, scalar2=None, op0=ALU.add
-            )
-            rstd[h] = keep.tile([P, 1], F32, name="rstd_%d" % h)
-            nc.gpsimd.tensor_tensor(out=rstd[h][:], in0=var_eps[:], in1=neg_half[:], op=ALU.pow)
-            minus_mean_gamma[h] = keep.tile([P, 1], F32, name="minus_mean_gamma_%d" % h)
-            nc.vector.scalar_tensor_tensor(
-                out=minus_mean_gamma[h][:],
-                in0=mean_var[h][:, 0:1],
-                scalar=-1.0,
-                in1=gamma_beta[:, h : h + 1],
-                op0=ALU.mult,
+                out=y[h][:],
+                in0=y[h][:],
+                scalar1=mean_var[:, h, 0:1],
+                scalar2=gamma_beta[:, h : h + 1],
+                op0=ALU.subtract,
                 op1=ALU.mult,
             )
-        by_half = out.rearrange("(it p) (h c) -> h p it c", p=P, c=P)
-        for h in range(COL_HALVES):
-            gain = keep.tile([P, 1], F32, name="gain_%d" % h)
-            nc.vector.tensor_tensor(out=gain[:], in0=rstd[h][:], in1=gamma_beta[:, h : h + 1], op=ALU.mult)
-            shift = keep.tile([P, 1], F32, name="shift_%d" % h)
-            nc.vector.scalar_tensor_tensor(
-                out=shift[:],
-                in0=minus_mean_gamma[h][:],
-                scalar=rstd[h][:],
-                in1=gamma_beta[:, COL_HALVES + h : COL_HALVES + h + 1],
-                op0=ALU.mult,
-                op1=ALU.add,
+        for h in halves:
+            nc.scalar.activation(
+                out=y[h][:],
+                in_=y[h][:],
+                func=ACT.Sigmoid,
+                bias=gamma_beta[:, COL_HALVES + h : COL_HALVES + h + 1],
+                scale=rstd[:, h : h + 1],
             )
-            nc.scalar.activation(out=y[h][:], in_=y[h][:], func=ACT.Sigmoid, bias=shift[:], scale=gain[:])
 
-            result = keep.tile([P, ITEM_TILES, P], F32, name="result_%d" % h)
+        by_half = out.rearrange("(it p) (h c) -> h p it c", p=P, c=P)
+        for h in halves:
+            result = keep.tile([P, ITEM_TILES, P], F32, name="result_%d" % h, align_bytes=256)
             for it in range(ITEM_TILES):
                 back = turn.tile([P, P], F32, tag="turned")
                 nc.tensor.transpose(back[:], y[h][:, it * P : (it + 1) * P], ident[:])

import concourse.mybir as mybir
from concourse.masks import make_identity

FLOPS = 2 * 2 * 256 * 16384 * 256

F32 = mybir.dt.float32
BF16 = mybir.dt.bfloat16
I32 = mybir.dt.int32
U32 = mybir.dt.uint32
U8 = mybir.dt.uint8
FP8X4 = mybir.dt.float8_e4m3fn_x4
ALU = mybir.AluOpType
ACT = mybir.ActivationFunctionType

P = 128
ITEMS = 256
ITEM_TILES = ITEMS // P
FEATURES = 16384
COLS = 256
COL_HALVES = COLS // P
GROUP = 4 * P
GROUPS = FEATURES // GROUP
GROUP_WORDS = GROUP // 2
CHUNK = 4096
CHUNKS = FEATURES // CHUNK
CHUNK_GROUPS = CHUNK // GROUP
BANK_GROUPS = 2
PIECE_GROUPS = 4
SCALE_ROWS = 4
BN_EPS = 1e-5

SELF = 0
NEIGH = 1


def tile_dogtaitujuanji_pb_k_kernel(
    tc, h_sage, w1b_words, w1b_scales, w2b_words, w2b_scales, gamma, beta, out
):
    nc = tc.nc
    weight_words = {SELF: w2b_words, NEIGH: w1b_words}
    weight_scales = {SELF: w2b_scales, NEIGH: w1b_scales}

    with tc.tile_pool(name="keep", bufs=1) as keep, tc.tile_pool(name="hops", bufs=4) as hops, tc.tile_pool(
        name="stage", bufs=4
    ) as stage, tc.tile_pool(name="weights", bufs=8) as weights, tc.psum_pool(
        name="sums", bufs=1
    ) as sums, tc.psum_pool(name="turn", bufs=4) as turn:
        ident = keep.tile([P, P], F32)
        make_identity(nc, ident[:])

        zero_col = keep.tile([P, 1], F32)
        nc.vector.memset(zero_col[:], 0.0)
        table_warm = keep.tile([P, 1], F32)
        nc.scalar.activation(out=table_warm[:], in_=zero_col[:], func=ACT.Sigmoid)

        neg_half = keep.tile([P, COL_HALVES], F32)
        nc.vector.memset(neg_half[:], -0.5)

        rows_bf = keep.tile([P, P], BF16)
        nc.vector.memset(rows_bf[:], 0.0)

        w_planes = keep.tile([P, GROUPS, COLS], U8, align_bytes=256)
        nc.vector.memset(w_planes[:].bitcast(I32), 0)
        scale_rows = [(operand, q) for operand in (SELF, NEIGH) for q in range(4 * SCALE_ROWS)]

        def load_scale_rows(rows):
            for operand, q in rows:
                p = 32 * (q // SCALE_ROWS) + q % SCALE_ROWS + SCALE_ROWS * operand
                nc.sync.dma_start(
                    out=w_planes[p : p + 1, :, :].bitcast(I32),
                    in_=weight_scales[operand][:, q : q + 1, :].rearrange("g q c -> q g c").bitcast(I32),
                )

        x_codes = {}
        x_planes = {}
        for operand in (SELF, NEIGH):
            for c in range(CHUNKS):
                x_codes[operand, c] = keep.tile(
                    [P, CHUNK_GROUPS, ITEMS], U32, name="x_codes_%d_%d" % (operand, c), align_bytes=256
                )
                x_planes[operand, c] = keep.tile(
                    [P, CHUNK_GROUPS, ITEMS], U8, name="x_planes_%d_%d" % (operand, c), align_bytes=256
                )

        for c in range(CHUNKS):
            features = slice(c * CHUNK, (c + 1) * CHUNK)
            for it in range(ITEM_TILES):
                items = slice(it * P, (it + 1) * P)
                neighbours = hops.tile([P, 2, CHUNK], BF16, align_bytes=256)
                nc.sync.dma_start(out=neighbours[:], in_=h_sage[items, 1:3, features])
                load_scale_rows(scale_rows[:4])
                scale_rows = scale_rows[4:]
                own = hops.tile([P, CHUNK], BF16, align_bytes=256)
                nc.sync.dma_start(out=own[:], in_=h_sage[items, 0, features])

                nc.vector.tensor_tensor(
                    out=neighbours[:, 0, :], in0=neighbours[:, 0, :], in1=neighbours[:, 1, :], op=ALU.add
                )

                for operand, values in ((SELF, own[:]), (NEIGH, neighbours[:, 0, :])):
                    words = values.bitcast(F32)
                    for first in range(0, CHUNK_GROUPS, BANK_GROUPS):
                        turned = turn.tile([P, BANK_GROUPS, 2, P], F32)
                        for j in range(BANK_GROUPS):
                            start_word = (first + j) * GROUP_WORDS
                            for u in range(2):
                                nc.tensor.transpose(
                                    turned[:, j, u, :],
                                    words[:, start_word + u : start_word + GROUP_WORDS : 2],
                                    ident[:],
                                )
                        grouped = stage.tile([P, BANK_GROUPS, 4 * P], BF16, align_bytes=256)
                        nc.scalar.copy(
                            out=grouped[:].bitcast(F32).rearrange("p j (i u) -> p j i u", u=2),
                            in_=turned[:].rearrange("p j u i -> p j i u"),
                        )
                        for j in range(BANK_GROUPS):
                            nc.vector.quantize_mx(
                                out=x_codes[operand, c][:, first + j, items].bitcast(FP8X4),
                                scales=x_planes[operand, c][:, first + j, items],
                                in_=grouped[:, j, :],
                            )

        nc.sync.dma_start(out=rows_bf[0:COL_HALVES, :], in_=gamma.rearrange("(h c) -> h c", h=COL_HALVES))
        nc.sync.dma_start(
            out=rows_bf[COL_HALVES : 2 * COL_HALVES, :], in_=beta.rearrange("(h c) -> h c", h=COL_HALVES)
        )
        rows_f32 = keep.tile([P, P], F32)
        nc.vector.tensor_copy(out=rows_f32[:], in_=rows_bf[:])
        cols_ps = turn.tile([P, P], F32, tag="turned")
        nc.tensor.transpose(cols_ps[:], rows_f32[:], ident[:])
        gamma_beta = keep.tile([P, 2 * COL_HALVES], F32)
        nc.vector.tensor_copy(out=gamma_beta[:], in_=cols_ps[:, 0 : 2 * COL_HALVES])

        product = {}
        for operand in (SELF, NEIGH):
            for h in range(COL_HALVES):
                product[operand, h] = sums.tile([P, ITEMS], F32, name="product_%d_%d" % (operand, h))

        self_sb = keep.tile([P, COL_HALVES, ITEMS], F32)
        pieces = [(operand, first, PIECE_GROUPS) for operand in (SELF, NEIGH) for first in range(0, GROUPS, PIECE_GROUPS)]
        operand, first, count = pieces[-1]
        pieces[-1:] = [(operand, first, count // 2), (operand, first + count // 2, count // 2)]
        for operand, first, count in pieces:
            piece = weights.tile([P, PIECE_GROUPS, COLS], U32, align_bytes=256)
            nc.sync.dma_start(
                out=piece[:, 0:count, :].bitcast(I32),
                in_=weight_words[operand][first : first + count]
                .rearrange("g p c t -> p g (c t)")
                .bitcast(I32),
            )
            for h in range(COL_HALVES):
                cols = slice(h * P, (h + 1) * P)
                for j in range(count):
                    g = first + j
                    nc.tensor.matmul_mx(
                        out=product[operand, h][:],
                        lhsT=piece[:, j, cols].bitcast(FP8X4),
                        lhsT_scale=w_planes[SCALE_ROWS * operand : P, g, cols],
                        rhs=x_codes[operand, g // CHUNK_GROUPS][:, g % CHUNK_GROUPS, :].bitcast(FP8X4),
                        rhs_scale=x_planes[operand, g // CHUNK_GROUPS][:, g % CHUNK_GROUPS, :],
                        start=(g == 0),
                        stop=(g == GROUPS - 1),
                    )
            if operand == SELF and first + count == GROUPS:
                for h in range(COL_HALVES):
                    nc.scalar.copy(out=self_sb[:, h, :], in_=product[SELF, h][:])

        y = {}
        stats = {}
        mean_var = keep.tile([P, COL_HALVES, 2], F32)
        var_eps = keep.tile([P, COL_HALVES], F32)
        rstd = keep.tile([P, COL_HALVES], F32)
        halves = range(COL_HALVES)
        for h in halves:
            y[h] = keep.tile([P, ITEMS], F32, name="y_%d" % h)
            nc.vector.scalar_tensor_tensor(
                out=y[h][:], in0=product[NEIGH, h][:], scalar=0.5, in1=self_sb[:, h, :], op0=ALU.mult, op1=ALU.add
            )
        for h in halves:
            stats[h] = keep.tile([P, 6], F32, name="stats_%d" % h)
            nc.vector.bn_stats(out=stats[h][:], in_=y[h][:])
        for h in halves:
            nc.vector.bn_aggr(out=mean_var[:, h, :], in_=stats[h][:])
        nc.vector.tensor_scalar(out=var_eps[:], in0=mean_var[:, :, 1], scalar1=BN_EPS, scalar2=None, op0=ALU.add)
        nc.gpsimd.tensor_tensor(out=rstd[:], in0=var_eps[:], in1=neg_half[:], op=ALU.pow)
        for h in halves:
            nc.vector.tensor_scalar(
                out=y[h][:],
                in0=y[h][:],
                scalar1=mean_var[:, h, 0:1],
                scalar2=gamma_beta[:, h : h + 1],
                op0=ALU.subtract,
                op1=ALU.mult,
            )
        for h in halves:
            nc.scalar.activation(
                out=y[h][:],
                in_=y[h][:],
                func=ACT.Sigmoid,
                bias=gamma_beta[:, COL_HALVES + h : COL_HALVES + h + 1],
                scale=rstd[:, h : h + 1],
            )

        by_half = out.rearrange("(it p) (h c) -> h p it c", p=P, c=P)
        for h in halves:
            result = keep.tile([P, ITEM_TILES, P], F32, name="result_%d" % h, align_bytes=256)
            for it in range(ITEM_TILES):
                back = turn.tile([P, P], F32, tag="turned")
                nc.tensor.transpose(back[:], y[h][:, it * P : (it + 1) * P], ident[:])
                if it == 0:
                    nc.vector.tensor_copy(out=result[:, it, :], in_=back[:])
                else:
                    nc.scalar.copy(out=result[:, it, :], in_=back[:])
            nc.sync.dma_start(out=by_half[h], in_=result[:])
